import numpy as np
import ml_dtypes


def mxq(x, axis, fmt="e4m3"):
    dtype, down = {"e4m3": (ml_dtypes.float8_e4m3fn, 7), "e5m2": (ml_dtypes.float8_e5m2, 14)}[fmt]
    v = np.moveaxis(np.asarray(x, np.float32).astype(ml_dtypes.bfloat16).astype(np.float64), axis, -1)
    blocks = v.reshape(v.shape[:-1] + (-1, 32))
    amax = np.abs(blocks).max(-1, keepdims=True)
    byte = np.maximum(np.where(amax > 0, np.frexp(amax)[1] - 1 + 127, 0) - down, 1)
    scale = np.exp2(byte - 127.0)
    codes = (blocks / scale).astype(np.float32).astype(dtype).astype(np.float64)
    return np.moveaxis((codes * scale).reshape(v.shape), -1, axis)


WIDE = False


def mx_kscale(k):
    if not WIDE:
        return np.ones(k)
    levels = np.array([10, -10, 5, -5, 0])
    a = np.random.permutation(np.resize(levels, k // 512 * 4)).reshape(k // 512, 4)
    idx = np.arange(k)
    return np.exp2(a[idx // 512, idx % 128 // 32])


BF16 = ml_dtypes.bfloat16


def bf(x):
    return np.asarray(x, np.float32).astype(BF16)


def f64(x):
    return np.asarray(x).astype(np.float64)


E2M1 = np.array([0.0, 0.5, 1.0, 1.5, 2.0, 3.0, 4.0, 6.0, -0.0, -0.5, -1.0, -1.5, -2.0, -3.0, -4.0, -6.0])


def pack_weight(w, fmt):
    k, n = w.shape
    w = f64(bf(w)).reshape(k // 32, 32, n)
    amax = np.abs(w).max(1)
    if fmt == "e4m3":
        byte = np.frexp(amax)[1] - 1 + 127 - 7
    else:
        mant, ex = np.frexp(amax / 6.0)
        byte = np.where(mant > 0.5, ex, ex - 1) + 127
    byte = np.clip(np.where(amax > 0, byte, 1), 1, 254)
    scaled = (w * np.exp2(127.0 - byte)[:, None, :]).reshape(k, n).astype(np.float32)
    by_word = np.ascontiguousarray(scaled.reshape(k // 512, 128, 4, n).transpose(0, 1, 3, 2))
    if fmt == "e4m3":
        words = by_word.astype(ml_dtypes.float8_e4m3fn).view(np.uint8)
    else:
        c = by_word.astype(ml_dtypes.float4_e2m1fn).view(np.uint8) & 0xF
        words = c[..., 0::2] | (c[..., 1::2] << 4)
    return np.ascontiguousarray(words), np.ascontiguousarray(byte.astype(np.uint8).reshape(k // 512, 16, n))


def unpack_weight(words, scales, fmt):
    g, p, n, _ = words.shape
    if fmt == "e4m3":
        vals = np.ascontiguousarray(words).view(ml_dtypes.float8_e4m3fn).astype(np.float64)
    else:
        nib = np.empty((g, p, n, 4), np.uint8)
        nib[..., 0::2] = words & 0xF
        nib[..., 1::2] = words >> 4
        vals = E2M1[nib]
    vals = vals * np.repeat(np.exp2(scales.astype(np.float64) - 127.0), 8, axis=1)[..., None]
    return vals.transpose(0, 1, 3, 2).reshape(g * 512, n)


B, N, I, O = 256, 24, 512, 256
WS = 0.7 / np.sqrt(I)
NP = N - 1


def setup_inputs():
    s = mx_kscale(I)
    x = bf((np.random.standard_normal((B, N, I)) * s).reshape(B, N * I))
    w_self = np.random.standard_normal((N, O, I)) * WS / s
    w_parent = np.random.standard_normal((NP, O, I)) * WS / s
    bias = bf(np.random.standard_normal(N * O) * 0.5)
    w_self_words, w_self_scales = pack_weight(w_self.swapaxes(1, 2).reshape(-1, O), "e4m3")
    w_parent_words, w_parent_scales = pack_weight(w_parent.swapaxes(1, 2).reshape(-1, O), "e4m3")
    return {"x": x,
            "w_self_words": w_self_words, "w_self_scales": w_self_scales,
            "w_parent_words": w_parent_words, "w_parent_scales": w_parent_scales,
            "bias": bias}


def reference(x, w_self_words, w_self_scales, w_parent_words, w_parent_scales, bias):
    xq = mxq(f64(x).reshape(B, N, I).transpose(1, 0, 2), 2, "e4m3")
    y_self = xq @ unpack_weight(w_self_words, w_self_scales, "e4m3").reshape(N, I, O)
    y_par = xq[:-1] @ unpack_weight(w_parent_words, w_parent_scales, "e4m3").reshape(NP, I, O)
    y = np.concatenate([y_self[:1], y_self[1:] + y_par], 0)
    return y.transpose(1, 0, 2).reshape(B, N * O) + f64(bias)

@@ -1,0 +1,172 @@
+from contextlib import ExitStack
+
+import concourse.mybir as mybir
+from concourse.masks import make_identity
+
+F32 = mybir.dt.float32
+BF16 = mybir.dt.bfloat16
+I32 = mybir.dt.int32
+U32 = mybir.dt.uint32
+U8 = mybir.dt.uint8
+FP8X4 = mybir.dt.float8_e4m3fn_x4
+
+P = 128
+HALVES = 2
+JOINTS = 24
+CH_IN = 512
+CH_OUT = 256
+PACK = 4
+WORDS_IN = CH_IN // 2
+BANK = 512
+PAIR = BANK // CH_OUT
+LOAD_JOINTS = 4
+LOADS = JOINTS // LOAD_JOINTS
+PAIRS = JOINTS // PAIR
+QUADRANTS = 4
+LIVE_ROWS = 4
+
+FLOPS = 2 * HALVES * P * CH_IN * CH_OUT * (2 * JOINTS - 1)
+
+
+def tile_skeletonlinear_pa_e_kernel(
+    tc, x, w_self_words, w_self_scales, w_parent_words, w_parent_scales, bias, out
+):
+    nc = tc.nc
+    with ExitStack() as ctx:
+        ctx.enter_context(tc.manual_schedule())
+        keep = ctx.enter_context(tc.tile_pool(name="keep", bufs=1))
+        stage = ctx.enter_context(tc.tile_pool(name="stage", bufs=3))
+        psum_xt = ctx.enter_context(tc.psum_pool(name="psum_xt", bufs=4))
+        psum_acc = ctx.enter_context(tc.psum_pool(name="psum_acc", bufs=3))
+        psum_bias = ctx.enter_context(tc.psum_pool(name="psum_bias", bufs=1))
+
+        x_view = x.rearrange("(h p) c -> p h c", p=P)
+        out_view = out.rearrange("(h p) c -> p h c", p=P)
+        self_view = w_self_words.bitcast(I32).rearrange("g p n o -> p g (n o)")
+        parent_view = w_parent_words.bitcast(I32).rearrange("g p n o -> p g (n o)")
+        x_tiles = []
+        self_tiles = []
+        parent_tiles = []
+        for c in range(LOADS):
+            first = c * LOAD_JOINTS
+            parents = min(LOAD_JOINTS, JOINTS - 1 - first)
+            x_sb = keep.tile([P, HALVES, LOAD_JOINTS * CH_IN], BF16, name="x%d" % c)
+            self_sb = keep.tile([P, LOAD_JOINTS, CH_OUT], I32, name="w_self%d" % c, align_bytes=64)
+            parent_sb = keep.tile([P, parents, CH_OUT], I32, name="w_parent%d" % c, align_bytes=64)
+            nc.sync.dma_start(out=x_sb[:], in_=x_view[:, :, first * CH_IN : (first + LOAD_JOINTS) * CH_IN])
+            nc.sync.dma_start(out=self_sb[:], in_=self_view[:, first : first + LOAD_JOINTS, :])
+            nc.sync.dma_start(out=parent_sb[:], in_=parent_view[:, first : first + parents, :])
+            x_tiles.append(x_sb)
+            self_tiles.append(self_sb)
+            parent_tiles.append(parent_sb)
+
+        bias_rows = keep.tile([P, BANK], BF16, name="bias_rows")
+        nc.vector.memset(bias_rows[:], 0.0)
+        nc.scalar.dma_start(out=bias_rows[0:PAIRS, :], in_=bias.rearrange("(j c) -> j c", c=BANK))
+
+        self_planes = keep.tile([P, JOINTS, CH_OUT], U8, name="self_planes", align_bytes=64)
+        parent_planes = keep.tile([P, JOINTS - 1, CH_OUT], U8, name="parent_planes", align_bytes=64)
+        ident_f32 = keep.tile([P, P], F32, name="ident_f32")
+        ident_bf16 = keep.tile([P, P], BF16, name="ident_bf16")
+        make_identity(nc, ident_f32[:])
+        make_identity(nc, ident_bf16[:])
+        for planes, scales in ((self_planes, w_self_scales), (parent_planes, w_parent_scales)):
+            nc.vector.memset(planes[:].bitcast(I32), 0)
+            rows = scales.bitcast(F32).rearrange("g (q r) n -> r q g n", r=LIVE_ROWS)
+            for r in range(LIVE_ROWS):
+                nc.gpsimd.dma_start(out=planes[r : P : P // QUADRANTS, :, :].bitcast(F32), in_=rows[r])
+
+        x_codes = []
+        x_planes = []
+        grouped_tiles = {}
+
+        def transpose_pair(pair):
+            grouped = stage.tile([P, PAIR * HALVES * P * PACK], BF16, name="grouped", align_bytes=64)
+            for i in range(PAIR):
+                joint = pair * PAIR + i
+                x_sb = x_tiles[joint // LOAD_JOINTS]
+                word0 = (joint % LOAD_JOINTS) * WORDS_IN
+                xt = psum_xt.tile([P, HALVES, 2, P], F32, name="xt")
+                for h in range(HALVES):
+                    words = x_sb[:, h, :].bitcast(F32)
+                    for u in range(2):
+                        nc.tensor.transpose(xt[:, h, u, :], words[:, word0 + u : word0 + WORDS_IN : 2], ident_f32[:])
+                width = HALVES * P * PACK
+                nc.scalar.copy(
+                    out=grouped[:, i * width : (i + 1) * width].bitcast(F32).rearrange(
+                        "p (h b u) -> p h b u", h=HALVES, u=2
+                    ),
+                    in_=xt[:].rearrange("p h u b -> p h b u"),
+                )
+            grouped_tiles[pair] = grouped
+
+        def quantise_pair(pair):
+            codes = keep.tile([P, PAIR * HALVES * P], U32, name="x_codes%d" % pair, align_bytes=64)
+            plane = keep.tile([P, PAIR * HALVES * P], U8, name="x_plane%d" % pair, align_bytes=64)
+            nc.vector.quantize_mx(out=codes[:].bitcast(FP8X4), scales=plane[:], in_=grouped_tiles[pair][:])
+            x_codes.append(codes)
+            x_planes.append(plane)
+
+        def product(acc, joint, h, w_tiles, w_planes, start, stop):
+            cols = slice(((joint % PAIR) * HALVES + h) * P, ((joint % PAIR) * HALVES + h + 1) * P)
+            nc.tensor.matmul_mx(
+                out=acc,
+                lhsT=x_codes[joint // PAIR][:, cols].bitcast(FP8X4),
+                lhsT_scale=x_planes[joint // PAIR][:, cols],
+                rhs=w_tiles[joint // LOAD_JOINTS][:, joint % LOAD_JOINTS, :].bitcast(FP8X4),
+                rhs_scale=w_planes[:, joint, :],
+                start=start,
+                stop=stop,
+            )
+
+        def spread_bias(pair):
+            bank = psum_bias.tile([P, BANK], F32, name="bias_bank")
+            nc.tensor.matmul(
+                out=bank[:],
+                lhsT=ident_bf16[:, pair : pair + 1].to_broadcast([P, P]),
+                rhs=bias_rows[:],
+                start=True,
+                stop=True,
+            )
+            spread = keep.tile([P, BANK], F32, name="bias_spread%d" % pair)
+            nc.scalar.copy(out=spread[:], in_=bank[:])
+            return spread
+
+        out_tiles = {}
+
+        def multiply_pair(pair):
+            spread = spread_bias(pair)
+            accs = []
+            for h in range(HALVES):
+                acc = psum_acc.tile([P, BANK], F32, name="acc")
+                for i in range(PAIR):
+                    joint = pair * PAIR + i
+                    group = acc[:, i * CH_OUT : (i + 1) * CH_OUT]
+                    product(group, joint, h, self_tiles, self_planes, True, joint == 0)
+                    if joint > 0:
+                        product(group, joint - 1, h, parent_tiles, parent_planes, False, True)
+                accs.append(acc)
+            return spread, accs
+
+        def finish_pair(pair, spread, accs):
+            c = pair * PAIR // LOAD_JOINTS
+            col0 = (pair * PAIR % LOAD_JOINTS) * CH_OUT
+            if col0 == 0:
+                out_tiles[c] = keep.tile([P, HALVES, LOAD_JOINTS * CH_OUT], F32, name="out%d" % c)
+            for h in range(HALVES):
+                nc.vector.tensor_tensor(
+                    out=out_tiles[c][:, h, col0 : col0 + BANK], in0=accs[h][:], in1=spread[:], op=mybir.AluOpType.add
+                )
+            if col0 + BANK == LOAD_JOINTS * CH_OUT:
+                width = LOAD_JOINTS * CH_OUT
+                nc.sync.dma_start(out=out_view[:, :, c * width : (c + 1) * width], in_=out_tiles[c][:])
+
+        transpose_pair(0)
+        quantise_pair(0)
+        for pair in range(PAIRS):
+            if pair + 1 < PAIRS:
+                transpose_pair(pair + 1)
+            spread, accs = multiply_pair(pair)
+            if pair + 1 < PAIRS:
+                quantise_pair(pair + 1)
+            finish_pair(pair, spread, accs)

@@ -24,6 +24,7 @@ LOADS = JOINTS // LOAD_JOINTS
 PAIRS = JOINTS // PAIR
 QUADRANTS = 4
 LIVE_ROWS = 4
+PARENT_ROW0 = 4
 
 FLOPS = 2 * HALVES * P * CH_IN * CH_OUT * (2 * JOINTS - 1)
 
@@ -64,17 +65,18 @@ def tile_skeletonlinear_pa_e_kernel(
         nc.vector.memset(bias_rows[:], 0.0)
         nc.scalar.dma_start(out=bias_rows[0:PAIRS, :], in_=bias.rearrange("(j c) -> j c", c=BANK))
 
-        self_planes = keep.tile([P, JOINTS, CH_OUT], U8, name="self_planes", align_bytes=64)
-        parent_planes = keep.tile([P, JOINTS - 1, CH_OUT], U8, name="parent_planes", align_bytes=64)
+        planes = keep.tile([P, JOINTS, CH_OUT], U8, name="planes", align_bytes=64)
         ident_f32 = keep.tile([P, P], F32, name="ident_f32")
         ident_bf16 = keep.tile([P, P], BF16, name="ident_bf16")
         make_identity(nc, ident_f32[:])
         make_identity(nc, ident_bf16[:])
-        for planes, scales in ((self_planes, w_self_scales), (parent_planes, w_parent_scales)):
-            nc.vector.memset(planes[:].bitcast(I32), 0)
+        nc.vector.memset(planes[:].bitcast(I32), 0)
+        for row0, count, scales in ((0, JOINTS, w_self_scales), (PARENT_ROW0, JOINTS - 1, w_parent_scales)):
             rows = scales.bitcast(F32).rearrange("g (q r) n -> r q g n", r=LIVE_ROWS)
             for r in range(LIVE_ROWS):
-                nc.gpsimd.dma_start(out=planes[r : P : P // QUADRANTS, :, :].bitcast(F32), in_=rows[r])
+                nc.gpsimd.dma_start(
+                    out=planes[row0 + r : P : P // QUADRANTS, 0:count, :].bitcast(F32), in_=rows[r]
+                )
 
         x_codes = []
         x_planes = []
@@ -107,14 +109,14 @@ def tile_skeletonlinear_pa_e_kernel(
             x_codes.append(codes)
             x_planes.append(plane)
 
-        def product(acc, joint, h, w_tiles, w_planes, start, stop):
+        def product(acc, joint, h, w_tiles, row0, start, stop):
             cols = slice(((joint % PAIR) * HALVES + h) * P, ((joint % PAIR) * HALVES + h + 1) * P)
             nc.tensor.matmul_mx(
                 out=acc,
                 lhsT=x_codes[joint // PAIR][:, cols].bitcast(FP8X4),
                 lhsT_scale=x_planes[joint // PAIR][:, cols],
                 rhs=w_tiles[joint // LOAD_JOINTS][:, joint % LOAD_JOINTS, :].bitcast(FP8X4),
-                rhs_scale=w_planes[:, joint, :],
+                rhs_scale=planes[row0:P, joint, :],
                 start=start,
                 stop=stop,
             )
@@ -142,9 +144,9 @@ def tile_skeletonlinear_pa_e_kernel(
                 for i in range(PAIR):
                     joint = pair * PAIR + i
                     group = acc[:, i * CH_OUT : (i + 1) * CH_OUT]
-                    product(group, joint, h, self_tiles, self_planes, True, joint == 0)
+                    product(group, joint, h, self_tiles, 0, True, joint == 0)
                     if joint > 0:
-                        product(group, joint - 1, h, parent_tiles, parent_planes, False, True)
+                        product(group, joint - 1, h, parent_tiles, PARENT_ROW0, False, True)
                 accs.append(acc)
             return spread, accs
 

@@ -18,6 +18,7 @@ CH_OUT = 256
 PACK = 4
 WORDS_IN = CH_IN // 2
 BANK = 512
+BANKS = 8
 PAIR = BANK // CH_OUT
 LOAD_JOINTS = 4
 LOADS = JOINTS // LOAD_JOINTS
@@ -37,9 +38,7 @@ def tile_skeletonlinear_pa_e_kernel(
         ctx.enter_context(tc.manual_schedule())
         keep = ctx.enter_context(tc.tile_pool(name="keep", bufs=1))
         stage = ctx.enter_context(tc.tile_pool(name="stage", bufs=3))
-        psum_xt = ctx.enter_context(tc.psum_pool(name="psum_xt", bufs=4))
-        psum_acc = ctx.enter_context(tc.psum_pool(name="psum_acc", bufs=3))
-        psum_bias = ctx.enter_context(tc.psum_pool(name="psum_bias", bufs=1))
+        psum = ctx.enter_context(tc.psum_pool(name="psum", bufs=BANKS))
 
         x_view = x.rearrange("(h p) c -> p h c", p=P)
         out_view = out.rearrange("(h p) c -> p h c", p=P)
@@ -50,14 +49,16 @@ def tile_skeletonlinear_pa_e_kernel(
         parent_tiles = []
         for c in range(LOADS):
             first = c * LOAD_JOINTS
-            parents = min(LOAD_JOINTS, JOINTS - 1 - first)
             x_sb = keep.tile([P, HALVES, LOAD_JOINTS * CH_IN], BF16, name="x%d" % c)
+            nc.sync.dma_start(out=x_sb[:], in_=x_view[:, :, first * CH_IN : (first + LOAD_JOINTS) * CH_IN])
+            x_tiles.append(x_sb)
+        for c in range(LOADS):
+            first = c * LOAD_JOINTS
+            parents = min(LOAD_JOINTS, JOINTS - 1 - first)
             self_sb = keep.tile([P, LOAD_JOINTS, CH_OUT], I32, name="w_self%d" % c, align_bytes=64)
             parent_sb = keep.tile([P, parents, CH_OUT], I32, name="w_parent%d" % c, align_bytes=64)
-            nc.sync.dma_start(out=x_sb[:], in_=x_view[:, :, first * CH_IN : (first + LOAD_JOINTS) * CH_IN])
             nc.sync.dma_start(out=self_sb[:], in_=self_view[:, first : first + LOAD_JOINTS, :])
             nc.sync.dma_start(out=parent_sb[:], in_=parent_view[:, first : first + parents, :])
-            x_tiles.append(x_sb)
             self_tiles.append(self_sb)
             parent_tiles.append(parent_sb)
 
@@ -80,7 +81,7 @@ def tile_skeletonlinear_pa_e_kernel(
 
         x_codes = []
         x_planes = []
-        grouped_tiles = {}
+        spreads = []
 
         def transpose_pair(pair):
             grouped = stage.tile([P, PAIR * HALVES * P * PACK], BF16, name="grouped", align_bytes=64)
@@ -88,7 +89,7 @@ def tile_skeletonlinear_pa_e_kernel(
                 joint = pair * PAIR + i
                 x_sb = x_tiles[joint // LOAD_JOINTS]
                 word0 = (joint % LOAD_JOINTS) * WORDS_IN
-                xt = psum_xt.tile([P, HALVES, 2, P], F32, name="xt")
+                xt = psum.tile([P, HALVES, 2, P], F32, name="bank")
                 for h in range(HALVES):
                     words = x_sb[:, h, :].bitcast(F32)
                     for u in range(2):
@@ -100,12 +101,25 @@ def tile_skeletonlinear_pa_e_kernel(
                     ),
                     in_=xt[:].rearrange("p h u b -> p h b u"),
                 )
-            grouped_tiles[pair] = grouped
+            return grouped
 
-        def quantise_pair(pair):
+        def spread_bias(pair):
+            bank = psum.tile([P, BANK], F32, name="bank")
+            nc.tensor.matmul(
+                out=bank[:],
+                lhsT=ident_bf16[:, pair : pair + 1].to_broadcast([P, P]),
+                rhs=bias_rows[:],
+                start=True,
+                stop=True,
+            )
+            spread = keep.tile([P, BANK], F32, name="bias_spread%d" % pair)
+            nc.vector.tensor_copy(out=spread[:], in_=bank[:])
+            spreads.append(spread)
+
+        def quantise_pair(pair, grouped):
             codes = keep.tile([P, PAIR * HALVES * P], U32, name="x_codes%d" % pair, align_bytes=64)
             plane = keep.tile([P, PAIR * HALVES * P], U8, name="x_plane%d" % pair, align_bytes=64)
-            nc.vector.quantize_mx(out=codes[:].bitcast(FP8X4), scales=plane[:], in_=grouped_tiles[pair][:])
+            nc.vector.quantize_mx(out=codes[:].bitcast(FP8X4), scales=plane[:], in_=grouped[:])
             x_codes.append(codes)
             x_planes.append(plane)
 
@@ -121,54 +135,31 @@ def tile_skeletonlinear_pa_e_kernel(
                 stop=stop,
             )
 
-        def spread_bias(pair):
-            bank = psum_bias.tile([P, BANK], F32, name="bias_bank")
-            nc.tensor.matmul(
-                out=bank[:],
-                lhsT=ident_bf16[:, pair : pair + 1].to_broadcast([P, P]),
-                rhs=bias_rows[:],
-                start=True,
-                stop=True,
-            )
-            spread = keep.tile([P, BANK], F32, name="bias_spread%d" % pair)
-            nc.scalar.copy(out=spread[:], in_=bank[:])
-            return spread
-
         out_tiles = {}
 
         def multiply_pair(pair):
-            spread = spread_bias(pair)
-            accs = []
+            c = pair * PAIR // LOAD_JOINTS
+            col0 = (pair * PAIR % LOAD_JOINTS) * CH_OUT
+            if col0 == 0:
+                out_tiles[c] = keep.tile([P, HALVES, LOAD_JOINTS * CH_OUT], F32, name="out%d" % c)
             for h in range(HALVES):
-                acc = psum_acc.tile([P, BANK], F32, name="acc")
+                acc = psum.tile([P, BANK], F32, name="bank")
                 for i in range(PAIR):
                     joint = pair * PAIR + i
                     group = acc[:, i * CH_OUT : (i + 1) * CH_OUT]
                     product(group, joint, h, self_tiles, 0, True, joint == 0)
                     if joint > 0:
                         product(group, joint - 1, h, parent_tiles, PARENT_ROW0, False, True)
-                accs.append(acc)
-            return spread, accs
-
-        def finish_pair(pair, spread, accs):
-            c = pair * PAIR // LOAD_JOINTS
-            col0 = (pair * PAIR % LOAD_JOINTS) * CH_OUT
-            if col0 == 0:
-                out_tiles[c] = keep.tile([P, HALVES, LOAD_JOINTS * CH_OUT], F32, name="out%d" % c)
-            for h in range(HALVES):
                 nc.vector.tensor_tensor(
-                    out=out_tiles[c][:, h, col0 : col0 + BANK], in0=accs[h][:], in1=spread[:], op=mybir.AluOpType.add
+                    out=out_tiles[c][:, h, col0 : col0 + BANK], in0=acc[:], in1=spreads[pair][:], op=mybir.AluOpType.add
                 )
             if col0 + BANK == LOAD_JOINTS * CH_OUT:
                 width = LOAD_JOINTS * CH_OUT
                 nc.sync.dma_start(out=out_view[:, :, c * width : (c + 1) * width], in_=out_tiles[c][:])
 
-        transpose_pair(0)
-        quantise_pair(0)
         for pair in range(PAIRS):
-            if pair + 1 < PAIRS:
-                transpose_pair(pair + 1)
-            spread, accs = multiply_pair(pair)
-            if pair + 1 < PAIRS:
-                quantise_pair(pair + 1)
-            finish_pair(pair, spread, accs)
+            grouped = transpose_pair(pair)
+            spread_bias(pair)
+            quantise_pair(pair, grouped)
+        for pair in range(PAIRS):
+            multiply_pair(pair)

@@ -22,6 +22,9 @@ BANKS = 8
 PAIR = BANK // CH_OUT
 LOAD_JOINTS = 4
 LOADS = JOINTS // LOAD_JOINTS
+X_JOINTS = 12
+GROUP = 4
+STORES = ((0, 12), (12, 8), (20, 4))
 PAIRS = JOINTS // PAIR
 QUADRANTS = 4
 LIVE_ROWS = 4
@@ -40,18 +43,18 @@ def tile_skeletonlinear_pa_e_kernel(
         stage = ctx.enter_context(tc.tile_pool(name="stage", bufs=3))
         psum = ctx.enter_context(tc.psum_pool(name="psum", bufs=BANKS))
 
-        x_view = x.rearrange("(h p) c -> p h c", p=P)
-        out_view = out.rearrange("(h p) c -> p h c", p=P)
+        x_view = x.rearrange("(h p) c -> h p c", p=P)
+        out_view = out.rearrange("(h p) c -> h p c", p=P)
         self_view = w_self_words.bitcast(I32).rearrange("g p n o -> p g (n o)")
         parent_view = w_parent_words.bitcast(I32).rearrange("g p n o -> p g (n o)")
-        x_tiles = []
+        x_tiles = {}
         self_tiles = []
         parent_tiles = []
-        for c in range(LOADS):
-            first = c * LOAD_JOINTS
-            x_sb = keep.tile([P, HALVES, LOAD_JOINTS * CH_IN], BF16, name="x%d" % c)
-            nc.sync.dma_start(out=x_sb[:], in_=x_view[:, :, first * CH_IN : (first + LOAD_JOINTS) * CH_IN])
-            x_tiles.append(x_sb)
+        for c in range(JOINTS // X_JOINTS):
+            for h in range(HALVES):
+                x_sb = keep.tile([P, X_JOINTS * CH_IN], BF16, name="x%d_%d" % (h, c))
+                nc.sync.dma_start(out=x_sb[:], in_=x_view[h, :, c * X_JOINTS * CH_IN : (c + 1) * X_JOINTS * CH_IN])
+                x_tiles[(h, c)] = x_sb
         for c in range(LOADS):
             first = c * LOAD_JOINTS
             parents = min(LOAD_JOINTS, JOINTS - 1 - first)
@@ -79,27 +82,26 @@ def tile_skeletonlinear_pa_e_kernel(
                     out=planes[row0 + r : P : P // QUADRANTS, 0:count, :].bitcast(F32), in_=rows[r]
                 )
 
-        x_codes = []
-        x_planes = []
+        x_codes = {}
+        x_planes = {}
         spreads = []
 
-        def transpose_pair(pair):
-            grouped = stage.tile([P, PAIR * HALVES * P * PACK], BF16, name="grouped", align_bytes=64)
-            for i in range(PAIR):
-                joint = pair * PAIR + i
-                x_sb = x_tiles[joint // LOAD_JOINTS]
-                word0 = (joint % LOAD_JOINTS) * WORDS_IN
-                xt = psum.tile([P, HALVES, 2, P], F32, name="bank")
-                for h in range(HALVES):
-                    words = x_sb[:, h, :].bitcast(F32)
+        def transpose_group(h, group):
+            grouped = stage.tile([P, GROUP * P * PACK], BF16, name="grouped", align_bytes=64)
+            width = PAIR * P * PACK
+            for i in range(GROUP // PAIR):
+                xt = psum.tile([P, PAIR, 2, P], F32, name="bank")
+                for j in range(PAIR):
+                    joint = group * GROUP + i * PAIR + j
+                    words = x_tiles[(h, joint // X_JOINTS)][:].bitcast(F32)
+                    word0 = (joint % X_JOINTS) * WORDS_IN
                     for u in range(2):
-                        nc.tensor.transpose(xt[:, h, u, :], words[:, word0 + u : word0 + WORDS_IN : 2], ident_f32[:])
-                width = HALVES * P * PACK
+                        nc.tensor.transpose(xt[:, j, u, :], words[:, word0 + u : word0 + WORDS_IN : 2], ident_f32[:])
                 nc.scalar.copy(
                     out=grouped[:, i * width : (i + 1) * width].bitcast(F32).rearrange(
-                        "p (h b u) -> p h b u", h=HALVES, u=2
+                        "p (j b u) -> p j b u", j=PAIR, u=2
                     ),
-                    in_=xt[:].rearrange("p h u b -> p h b u"),
+                    in_=xt[:].rearrange("p j u b -> p j b u"),
                 )
             return grouped
 
@@ -116,19 +118,19 @@ def tile_skeletonlinear_pa_e_kernel(
             nc.vector.tensor_copy(out=spread[:], in_=bank[:])
             spreads.append(spread)
 
-        def quantise_pair(pair, grouped):
-            codes = keep.tile([P, PAIR * HALVES * P], U32, name="x_codes%d" % pair, align_bytes=64)
-            plane = keep.tile([P, PAIR * HALVES * P], U8, name="x_plane%d" % pair, align_bytes=64)
+        def quantise_group(h, group, grouped):
+            codes = keep.tile([P, GROUP * P], U32, name="x_codes%d_%d" % (h, group), align_bytes=64)
+            plane = keep.tile([P, GROUP * P], U8, name="x_plane%d_%d" % (h, group), align_bytes=64)
             nc.vector.quantize_mx(out=codes[:].bitcast(FP8X4), scales=plane[:], in_=grouped[:])
-            x_codes.append(codes)
-            x_planes.append(plane)
+            x_codes[(h, group)] = codes
+            x_planes[(h, group)] = plane
 
         def product(acc, joint, h, w_tiles, row0, start, stop):
-            cols = slice(((joint % PAIR) * HALVES + h) * P, ((joint % PAIR) * HALVES + h + 1) * P)
+            cols = slice((joint % GROUP) * P, (joint % GROUP + 1) * P)
             nc.tensor.matmul_mx(
                 out=acc,
-                lhsT=x_codes[joint // PAIR][:, cols].bitcast(FP8X4),
-                lhsT_scale=x_planes[joint // PAIR][:, cols],
+                lhsT=x_codes[(h, joint // GROUP)][:, cols].bitcast(FP8X4),
+                lhsT_scale=x_planes[(h, joint // GROUP)][:, cols],
                 rhs=w_tiles[joint // LOAD_JOINTS][:, joint % LOAD_JOINTS, :].bitcast(FP8X4),
                 rhs_scale=planes[row0:P, joint, :],
                 start=start,
@@ -138,11 +140,15 @@ def tile_skeletonlinear_pa_e_kernel(
         out_tiles = {}
 
         def multiply_pair(pair):
-            c = pair * PAIR // LOAD_JOINTS
-            col0 = (pair * PAIR % LOAD_JOINTS) * CH_OUT
-            if col0 == 0:
-                out_tiles[c] = keep.tile([P, HALVES, LOAD_JOINTS * CH_OUT], F32, name="out%d" % c)
+            s = 0
+            for n in range(len(STORES)):
+                if STORES[n][0] <= pair * PAIR:
+                    s = n
+            first, count = STORES[s]
+            col0 = (pair * PAIR - first) * CH_OUT
             for h in range(HALVES):
+                if col0 == 0:
+                    out_tiles[(h, s)] = keep.tile([P, count * CH_OUT], F32, name="out%d_%d" % (h, s))
                 acc = psum.tile([P, BANK], F32, name="bank")
                 for i in range(PAIR):
                     joint = pair * PAIR + i
@@ -151,15 +157,20 @@ def tile_skeletonlinear_pa_e_kernel(
                     if joint > 0:
                         product(group, joint - 1, h, parent_tiles, PARENT_ROW0, False, True)
                 nc.vector.tensor_tensor(
-                    out=out_tiles[c][:, h, col0 : col0 + BANK], in0=acc[:], in1=spreads[pair][:], op=mybir.AluOpType.add
+                    out=out_tiles[(h, s)][:, col0 : col0 + BANK], in0=acc[:], in1=spreads[pair][:], op=mybir.AluOpType.add
                 )
-            if col0 + BANK == LOAD_JOINTS * CH_OUT:
-                width = LOAD_JOINTS * CH_OUT
-                nc.sync.dma_start(out=out_view[:, :, c * width : (c + 1) * width], in_=out_tiles[c][:])
+                if col0 + BANK == count * CH_OUT:
+                    nc.sync.dma_start(
+                        out=out_view[h, :, first * CH_OUT : (first + count) * CH_OUT], in_=out_tiles[(h, s)][:]
+                    )
 
-        for pair in range(PAIRS):
-            grouped = transpose_pair(pair)
-            spread_bias(pair)
-            quantise_pair(pair, grouped)
+        done = 0
+        for c in range(JOINTS // X_JOINTS):
+            for h in range(HALVES):
+                for group in range(c * X_JOINTS // GROUP, (c + 1) * X_JOINTS // GROUP):
+                    grouped = transpose_group(h, group)
+                    spread_bias(done)
+                    quantise_group(h, group, grouped)
+                    done += 1
         for pair in range(PAIRS):
             multiply_pair(pair)

@@ -43,6 +43,9 @@ def tile_skeletonlinear_pa_e_kernel(
         stage = ctx.enter_context(tc.tile_pool(name="stage", bufs=3))
         psum = ctx.enter_context(tc.psum_pool(name="psum", bufs=BANKS))
 
+        bias_rows = keep.tile([P, BANK], BF16, name="bias_rows")
+        nc.vector.memset(bias_rows[:], 0.0)
+
         x_view = x.rearrange("(h p) c -> h p c", p=P)
         out_view = out.rearrange("(h p) c -> h p c", p=P)
         self_view = w_self_words.bitcast(I32).rearrange("g p n o -> p g (n o)")
@@ -55,6 +58,8 @@ def tile_skeletonlinear_pa_e_kernel(
                 x_sb = keep.tile([P, X_JOINTS * CH_IN], BF16, name="x%d_%d" % (h, c))
                 nc.sync.dma_start(out=x_sb[:], in_=x_view[h, :, c * X_JOINTS * CH_IN : (c + 1) * X_JOINTS * CH_IN])
                 x_tiles[(h, c)] = x_sb
+                if (h, c) == (0, 0):
+                    nc.sync.dma_start(out=bias_rows[0:PAIRS, :], in_=bias.rearrange("(j c) -> j c", c=BANK))
         for c in range(LOADS):
             first = c * LOAD_JOINTS
             parents = min(LOAD_JOINTS, JOINTS - 1 - first)
@@ -64,10 +69,6 @@ def tile_skeletonlinear_pa_e_kernel(
             nc.sync.dma_start(out=parent_sb[:], in_=parent_view[:, first : first + parents, :])
             self_tiles.append(self_sb)
             parent_tiles.append(parent_sb)
-
-        bias_rows = keep.tile([P, BANK], BF16, name="bias_rows")
-        nc.vector.memset(bias_rows[:], 0.0)
-        nc.scalar.dma_start(out=bias_rows[0:PAIRS, :], in_=bias.rearrange("(j c) -> j c", c=BANK))
 
         planes = keep.tile([P, JOINTS, CH_OUT], U8, name="planes", align_bytes=64)
         ident_f32 = keep.tile([P, P], F32, name="ident_f32")

from contextlib import ExitStack

import concourse.mybir as mybir
from concourse.masks import make_identity

F32 = mybir.dt.float32
BF16 = mybir.dt.bfloat16
I32 = mybir.dt.int32
U32 = mybir.dt.uint32
U8 = mybir.dt.uint8
FP8X4 = mybir.dt.float8_e4m3fn_x4

P = 128
HALVES = 2
JOINTS = 24
CH_IN = 512
CH_OUT = 256
PACK = 4
WORDS_IN = CH_IN // 2
BANK = 512
BANKS = 8
PAIR = BANK // CH_OUT
LOAD_JOINTS = 4
LOADS = JOINTS // LOAD_JOINTS
X_JOINTS = 12
GROUP = 4
STORES = ((0, 12), (12, 8), (20, 4))
PAIRS = JOINTS // PAIR
QUADRANTS = 4
LIVE_ROWS = 4
PARENT_ROW0 = 4

FLOPS = 2 * HALVES * P * CH_IN * CH_OUT * (2 * JOINTS - 1)


def tile_skeletonlinear_pa_e_kernel(
    tc, x, w_self_words, w_self_scales, w_parent_words, w_parent_scales, bias, out
):
    nc = tc.nc
    with ExitStack() as ctx:
        ctx.enter_context(tc.manual_schedule())
        keep = ctx.enter_context(tc.tile_pool(name="keep", bufs=1))
        stage = ctx.enter_context(tc.tile_pool(name="stage", bufs=3))
        psum = ctx.enter_context(tc.psum_pool(name="psum", bufs=BANKS))

        bias_rows = keep.tile([P, BANK], BF16, name="bias_rows")
        nc.vector.memset(bias_rows[:], 0.0)

        x_view = x.rearrange("(h p) c -> h p c", p=P)
        out_view = out.rearrange("(h p) c -> h p c", p=P)
        self_view = w_self_words.bitcast(I32).rearrange("g p n o -> p g (n o)")
        parent_view = w_parent_words.bitcast(I32).rearrange("g p n o -> p g (n o)")
        x_tiles = {}
        self_tiles = []
        parent_tiles = []
        for c in range(JOINTS // X_JOINTS):
            for h in range(HALVES):
                x_sb = keep.tile([P, X_JOINTS * CH_IN], BF16, name="x%d_%d" % (h, c))
                nc.sync.dma_start(out=x_sb[:], in_=x_view[h, :, c * X_JOINTS * CH_IN : (c + 1) * X_JOINTS * CH_IN])
                x_tiles[(h, c)] = x_sb
                if (h, c) == (0, 0):
                    nc.sync.dma_start(out=bias_rows[0:PAIRS, :], in_=bias.rearrange("(j c) -> j c", c=BANK))
        for c in range(LOADS):
            first = c * LOAD_JOINTS
            parents = min(LOAD_JOINTS, JOINTS - 1 - first)
            self_sb = keep.tile([P, LOAD_JOINTS, CH_OUT], I32, name="w_self%d" % c, align_bytes=64)
            parent_sb = keep.tile([P, parents, CH_OUT], I32, name="w_parent%d" % c, align_bytes=64)
            nc.sync.dma_start(out=self_sb[:], in_=self_view[:, first : first + LOAD_JOINTS, :])
            nc.sync.dma_start(out=parent_sb[:], in_=parent_view[:, first : first + parents, :])
            self_tiles.append(self_sb)
            parent_tiles.append(parent_sb)

        planes = keep.tile([P, JOINTS, CH_OUT], U8, name="planes", align_bytes=64)
        ident_f32 = keep.tile([P, P], F32, name="ident_f32")
        ident_bf16 = keep.tile([P, P], BF16, name="ident_bf16")
        make_identity(nc, ident_f32[:])
        make_identity(nc, ident_bf16[:])
        nc.vector.memset(planes[:].bitcast(I32), 0)
        for row0, count, scales in ((0, JOINTS, w_self_scales), (PARENT_ROW0, JOINTS - 1, w_parent_scales)):
            rows = scales.bitcast(F32).rearrange("g (q r) n -> r q g n", r=LIVE_ROWS)
            for r in range(LIVE_ROWS):
                nc.gpsimd.dma_start(
                    out=planes[row0 + r : P : P // QUADRANTS, 0:count, :].bitcast(F32), in_=rows[r]
                )

        x_codes = {}
        x_planes = {}
        spreads = []

        def transpose_group(h, group):
            grouped = stage.tile([P, GROUP * P * PACK], BF16, name="grouped", align_bytes=64)
            width = PAIR * P * PACK
            for i in range(GROUP // PAIR):
                xt = psum.tile([P, PAIR, 2, P], F32, name="bank")
                for j in range(PAIR):
                    joint = group * GROUP + i * PAIR + j
                    words = x_tiles[(h, joint // X_JOINTS)][:].bitcast(F32)
                    word0 = (joint % X_JOINTS) * WORDS_IN
                    for u in range(2):
                        nc.tensor.transpose(xt[:, j, u, :], words[:, word0 + u : word0 + WORDS_IN : 2], ident_f32[:])
                nc.scalar.copy(
                    out=grouped[:, i * width : (i + 1) * width].bitcast(F32).rearrange(
                        "p (j b u) -> p j b u", j=PAIR, u=2
                    ),
                    in_=xt[:].rearrange("p j u b -> p j b u"),
                )
            return grouped

        def spread_bias(pair):
            bank = psum.tile([P, BANK], F32, name="bank")
            nc.tensor.matmul(
                out=bank[:],
                lhsT=ident_bf16[:, pair : pair + 1].to_broadcast([P, P]),
                rhs=bias_rows[:],
                start=True,
                stop=True,
            )
            spread = keep.tile([P, BANK], F32, name="bias_spread%d" % pair)
            nc.vector.tensor_copy(out=spread[:], in_=bank[:])
            spreads.append(spread)

        def quantise_group(h, group, grouped):
            codes = keep.tile([P, GROUP * P], U32, name="x_codes%d_%d" % (h, group), align_bytes=64)
            plane = keep.tile([P, GROUP * P], U8, name="x_plane%d_%d" % (h, group), align_bytes=64)
            nc.vector.quantize_mx(out=codes[:].bitcast(FP8X4), scales=plane[:], in_=grouped[:])
            x_codes[(h, group)] = codes
            x_planes[(h, group)] = plane

        def product(acc, joint, h, w_tiles, row0, start, stop):
            cols = slice((joint % GROUP) * P, (joint % GROUP + 1) * P)
            nc.tensor.matmul_mx(
                out=acc,
                lhsT=x_codes[(h, joint // GROUP)][:, cols].bitcast(FP8X4),
                lhsT_scale=x_planes[(h, joint // GROUP)][:, cols],
                rhs=w_tiles[joint // LOAD_JOINTS][:, joint % LOAD_JOINTS, :].bitcast(FP8X4),
                rhs_scale=planes[row0:P, joint, :],
                start=start,
                stop=stop,
            )

        out_tiles = {}

        def multiply_pair(pair):
            s = 0
            for n in range(len(STORES)):
                if STORES[n][0] <= pair * PAIR:
                    s = n
            first, count = STORES[s]
            col0 = (pair * PAIR - first) * CH_OUT
            for h in range(HALVES):
                if col0 == 0:
                    out_tiles[(h, s)] = keep.tile([P, count * CH_OUT], F32, name="out%d_%d" % (h, s))
                acc = psum.tile([P, BANK], F32, name="bank")
                for i in range(PAIR):
                    joint = pair * PAIR + i
                    group = acc[:, i * CH_OUT : (i + 1) * CH_OUT]
                    product(group, joint, h, self_tiles, 0, True, joint == 0)
                    if joint > 0:
                        product(group, joint - 1, h, parent_tiles, PARENT_ROW0, False, True)
                nc.vector.tensor_tensor(
                    out=out_tiles[(h, s)][:, col0 : col0 + BANK], in0=acc[:], in1=spreads[pair][:], op=mybir.AluOpType.add
                )
                if col0 + BANK == count * CH_OUT:
                    nc.sync.dma_start(
                        out=out_view[h, :, first * CH_OUT : (first + count) * CH_OUT], in_=out_tiles[(h, s)][:]
                    )

        done = 0
        for c in range(JOINTS // X_JOINTS):
            for h in range(HALVES):
                for group in range(c * X_JOINTS // GROUP, (c + 1) * X_JOINTS // GROUP):
                    grouped = transpose_group(h, group)
                    spread_bias(done)
                    quantise_group(h, group, grouped)
                    done += 1
        for pair in range(PAIRS):
            multiply_pair(pair)
